import numpy as np
import ml_dtypes


def mxq(x, axis, fmt="e4m3"):
    dtype, down = {"e4m3": (ml_dtypes.float8_e4m3fn, 7), "e5m2": (ml_dtypes.float8_e5m2, 14)}[fmt]
    v = np.moveaxis(np.asarray(x, np.float32).astype(ml_dtypes.bfloat16).astype(np.float64), axis, -1)
    blocks = v.reshape(v.shape[:-1] + (-1, 32))
    amax = np.abs(blocks).max(-1, keepdims=True)
    byte = np.maximum(np.where(amax > 0, np.frexp(amax)[1] - 1 + 127, 0) - down, 1)
    scale = np.exp2(byte - 127.0)
    codes = (blocks / scale).astype(np.float32).astype(dtype).astype(np.float64)
    return np.moveaxis((codes * scale).reshape(v.shape), -1, axis)


WIDE = False


def mx_kscale(k):
    if not WIDE:
        return np.ones(k)
    levels = np.array([10, -10, 5, -5, 0])
    a = np.random.permutation(np.resize(levels, k // 512 * 4)).reshape(k // 512, 4)
    idx = np.arange(k)
    return np.exp2(a[idx // 512, idx % 128 // 32])


BF16 = ml_dtypes.bfloat16


def bf(x):
    return np.asarray(x, np.float32).astype(BF16)


def f64(x):
    return np.asarray(x).astype(np.float64)


B, N, D, E, S, H = 2, 128, 128, 4, 128, 1024


def gelu_tanh(v):
    return 0.5 * v * (1.0 + np.tanh(np.sqrt(2.0 / np.pi) * (v + 0.044715 * v**3)))


def setup_inputs():
    t = mx_kscale(H)
    return {"h": bf(gelu_tanh(np.random.standard_normal((B, E, S, H)) * 0.9) * t),
            "w2": bf(np.random.standard_normal((E, H, D)) * 3.0 / np.sqrt(H) / t[:, None]),
            "b2": bf(np.random.standard_normal((E, D)) * 0.3),
            "x": bf(np.random.standard_normal((B, N, D))),
            "phi": bf(np.random.standard_normal((E, S, D)) * 2.0 / np.sqrt(D))}


def reference(h, w2, b2, x, phi):
    y = (mxq(f64(h), 3, "e4m3") @ mxq(f64(w2), 1, "e4m3")) + f64(b2)[None, :, None, :]
    logits = f64(x) @ f64(phi).reshape(E * S, D).T
    p = np.exp(logits - logits.max(2, keepdims=True))
    return (mxq(p, 2, "e4m3") @ mxq(y.reshape(B, E * S, D), 1, "e4m3")) / p.sum(2, keepdims=True)

@@ -1,0 +1,185 @@
+from contextlib import ExitStack
+
+import concourse.mybir as mybir
+from concourse.masks import make_identity
+
+F32 = mybir.dt.float32
+BF16 = mybir.dt.bfloat16
+U32 = mybir.dt.uint32
+U8 = mybir.dt.uint8
+FP8X4 = mybir.dt.float8_e4m3fn_x4
+ALU = mybir.AluOpType
+ACT = mybir.ActivationFunctionType
+
+P = 128
+B, E, S, H, D, N = 2, 4, 128, 1024, 128, 128
+PACK = 4
+K_PASS = P * PACK
+PASSES = H // K_PASS
+HALVES = 2
+
+FLOPS = 2 * (B * E * S * H * D + B * N * D * E * S + B * N * E * S * D)
+
+
+def tile_mixtureexpertsmlp_pb_s_kernel(tc, h, w2, b2, x, phi, out):
+    nc = tc.nc
+    with ExitStack() as ctx:
+        const = ctx.enter_context(tc.tile_pool(name="const", bufs=1))
+        loads = ctx.enter_context(tc.tile_pool(name="loads", bufs=1))
+        work = ctx.enter_context(tc.tile_pool(name="work", bufs=1))
+        ps_h = ctx.enter_context(tc.psum_pool(name="ps_h", bufs=3))
+        ps_y = ctx.enter_context(tc.psum_pool(name="ps_y", bufs=1))
+        ps_misc = ctx.enter_context(tc.psum_pool(name="ps_misc", bufs=3))
+
+        phi_sb = loads.tile([P, E, D], BF16)
+        nc.sync.dma_start(out=phi_sb[:], in_=phi.rearrange("e s d -> s e d"))
+        x_sb = loads.tile([P, B, D], BF16)
+        nc.sync.dma_start(out=x_sb[:], in_=x.rearrange("b n d -> n b d"))
+        bias_sb = loads.tile([P, E * D], BF16)
+        nc.gpsimd.dma_start(out=bias_sb[:], in_=b2.rearrange("e d -> (e d)").partition_broadcast(P))
+        w2_raw = []
+        h_sb = []
+        for e in range(E):
+            raw = loads.tile([P, PASSES, PACK, D], BF16, name="w2_raw_%d" % e)
+            nc.sync.dma_start(
+                out=raw[:].rearrange("q g (u c) d -> q (g u) (c d)", c=2),
+                in_=w2[e].rearrange("(j q c) d -> q j (c d)", q=P, c=2),
+            )
+            w2_raw.append(raw)
+            for b in range(B):
+                rows = loads.tile([P, H], BF16, name="h_sb_%d_%d" % (b, e))
+                nc.sync.dma_start(out=rows[:], in_=h[b, e])
+                h_sb.append(rows)
+
+        ident_bf = const.tile([P, P], BF16)
+        make_identity(nc, ident_bf[:])
+        ident_f32 = const.tile([P, P], F32)
+        make_identity(nc, ident_f32[:])
+        warm = const.tile([P, 1], F32)
+        nc.vector.memset(warm[:], 0.0)
+        nc.scalar.activation(out=warm[:], in_=warm[:], func=ACT.Exp)
+
+        xphi_ps = ps_misc.tile([P, B + E, P], BF16, tag="misc")
+        for b in range(B):
+            nc.tensor.transpose(xphi_ps[:, b, :], x_sb[:, b, :], ident_bf[:])
+        for e in range(E):
+            nc.tensor.transpose(xphi_ps[:, B + e, :], phi_sb[:, e, :], ident_bf[:])
+        xphi_t = work.tile([P, B + E, P], BF16)
+        nc.vector.tensor_copy(out=xphi_t[:], in_=xphi_ps[:])
+
+        p_codes = []
+        p_scales = []
+        inv_sum = []
+        for b in range(B):
+            logits = ps_misc.tile([P, E * S], F32, tag="misc", name="logits_%d" % b)
+            nc.tensor.matmul(
+                out=logits[:],
+                lhsT=xphi_t[:, b, :],
+                rhs=xphi_t[:, B:, :].rearrange("d e s -> d (e s)"),
+                start=True,
+                stop=True,
+            )
+            neg_max = work.tile([P, 1], F32, name="neg_max_%d" % b)
+            nc.vector.tensor_reduce(
+                out=neg_max[:], in_=logits[:], axis=mybir.AxisListType.X, op=ALU.max, negate=True
+            )
+            p_sb = work.tile([P, E, S], BF16, name="p_sb_%d" % b)
+            p_sum = work.tile([P, 1], F32, name="p_sum_%d" % b)
+            nc.scalar.activation(
+                out=p_sb[:].rearrange("n e s -> n (e s)"),
+                in_=logits[:],
+                func=ACT.Exp,
+                bias=neg_max[:],
+                scale=1.0,
+                accum_out=p_sum[:],
+            )
+            inv = work.tile([P, 1], F32, name="inv_sum_%d" % b)
+            nc.vector.reciprocal(out=inv[:], in_=p_sum[:])
+            inv_sum.append(inv)
+
+            p_ps = ps_misc.tile([P, E, N], BF16, tag="misc", name="p_ps_%d" % b)
+            for e in range(E):
+                nc.tensor.transpose(p_ps[:, e, :], p_sb[:, e, :], ident_bf[:])
+            p_grouped = work.tile([P, N, PACK], BF16, name="p_grouped_%d" % b, align_bytes=64)
+            nc.vector.tensor_copy(out=p_grouped[:], in_=p_ps[:].rearrange("s e n -> s n e"))
+            codes = work.tile([P, N], U32, name="p_codes_%d" % b, align_bytes=64)
+            scales = work.tile([P, N], U8, name="p_scales_%d" % b, align_bytes=64)
+            nc.vector.quantize_mx(
+                out=codes[:].bitcast(FP8X4),
+                scales=scales[:],
+                in_=p_grouped[:].rearrange("s n e -> s (n e)"),
+            )
+            p_codes.append(codes)
+            p_scales.append(scales)
+
+        y_ps = []
+        for b in range(B):
+            y_ps.append(ps_y.tile([P, E, D], F32, name="y_ps_%d" % b))
+        for e in range(E):
+            w2_grouped = work.tile([P, PASSES, D, PACK], BF16, name="w2_grouped_%d" % e, align_bytes=64)
+            nc.vector.tensor_copy(out=w2_grouped[:], in_=w2_raw[e][:].rearrange("q g t d -> q g d t"))
+            w2_codes = work.tile([P, PASSES, D], U32, name="w2_codes_%d" % e, align_bytes=64)
+            w2_scales = work.tile([P, PASSES, D], U8, name="w2_scales_%d" % e, align_bytes=64)
+            nc.vector.quantize_mx(
+                out=w2_codes[:].rearrange("q g d -> q (g d)").bitcast(FP8X4),
+                scales=w2_scales[:].rearrange("q g d -> q (g d)"),
+                in_=w2_grouped[:].rearrange("q g d t -> q (g d t)"),
+            )
+            for b in range(B):
+                words = h_sb[e * B + b][:].bitcast(F32)
+                h_ps = ps_h.tile([P, PASSES * HALVES, S], F32, tag="h_ps")
+                for j in range(PASSES * HALVES):
+                    nc.tensor.transpose(h_ps[:, j, :], words[:, j * P : (j + 1) * P], ident_f32[:])
+                h_grouped = work.tile([P, PASSES * S * PACK], BF16, name="h_grouped_%d_%d" % (b, e), align_bytes=64)
+                nc.scalar.copy(
+                    out=h_grouped[:].bitcast(F32).rearrange("q (g s u) -> q g s u", g=PASSES, u=HALVES),
+                    in_=h_ps[:].rearrange("q (g u) s -> q g s u", u=HALVES),
+                )
+                h_codes = work.tile([P, PASSES, S], U32, name="h_codes_%d_%d" % (b, e), align_bytes=64)
+                h_scales = work.tile([P, PASSES, S], U8, name="h_scales_%d_%d" % (b, e), align_bytes=64)
+                nc.vector.quantize_mx(
+                    out=h_codes[:].rearrange("q g s -> q (g s)").bitcast(FP8X4),
+                    scales=h_scales[:].rearrange("q g s -> q (g s)"),
+                    in_=h_grouped[:],
+                )
+                for g in range(PASSES):
+                    nc.tensor.matmul_mx(
+                        out=y_ps[b][:, e, :],
+                        lhsT=h_codes[:, g, :].bitcast(FP8X4),
+                        lhsT_scale=h_scales[:, g, :],
+                        rhs=w2_codes[:, g, :].bitcast(FP8X4),
+                        rhs_scale=w2_scales[:, g, :],
+                        start=(g == 0),
+                        stop=(g == PASSES - 1),
+                    )
+
+        for b in range(B):
+            y_grouped = work.tile([P, D, PACK], BF16, name="y_grouped_%d" % b, align_bytes=64)
+            nc.vector.tensor_tensor(
+                out=y_grouped[:],
+                in0=y_ps[b][:].rearrange("s e d -> s d e"),
+                in1=bias_sb[:].rearrange("s (e d) -> s d e", e=E),
+                op=ALU.add,
+            )
+            y_codes = work.tile([P, D], U32, name="y_codes_%d" % b, align_bytes=64)
+            y_scales = work.tile([P, D], U8, name="y_scales_%d" % b, align_bytes=64)
+            nc.vector.quantize_mx(
+                out=y_codes[:].bitcast(FP8X4),
+                scales=y_scales[:],
+                in_=y_grouped[:].rearrange("s d e -> s (d e)"),
+            )
+            o_ps = ps_misc.tile([P, D], F32, tag="misc", name="o_ps_%d" % b)
+            nc.tensor.matmul_mx(
+                out=o_ps[:],
+                lhsT=p_codes[b][:].bitcast(FP8X4),
+                lhsT_scale=p_scales[b][:],
+                rhs=y_codes[:].bitcast(FP8X4),
+                rhs_scale=y_scales[:],
+                start=True,
+                stop=True,
+            )
+            o_sb = work.tile([P, D], F32, name="o_sb_%d" % b)
+            nc.vector.tensor_scalar(
+                out=o_sb[:], in0=o_ps[:], scalar1=inv_sum[b][:], scalar2=None, op0=ALU.mult
+            )
+            nc.sync.dma_start(out=out[b], in_=o_sb[:])

@@ -17,6 +17,8 @@ PACK = 4
 K_PASS = P * PACK
 PASSES = H // K_PASS
 HALVES = 2
+LOGITS_ROUND = 0
+P_ROUND = 1
 
 FLOPS = 2 * (B * E * S * H * D + B * N * D * E * S + B * N * E * S * D)
 
@@ -24,149 +26,188 @@ FLOPS = 2 * (B * E * S * H * D + B * N * D * E * S + B * N * E * S * D)
 def tile_mixtureexpertsmlp_pb_s_kernel(tc, h, w2, b2, x, phi, out):
     nc = tc.nc
     with ExitStack() as ctx:
+        ctx.enter_context(tc.manual_schedule())
         const = ctx.enter_context(tc.tile_pool(name="const", bufs=1))
         loads = ctx.enter_context(tc.tile_pool(name="loads", bufs=1))
         work = ctx.enter_context(tc.tile_pool(name="work", bufs=1))
-        ps_h = ctx.enter_context(tc.psum_pool(name="ps_h", bufs=3))
+        ps_h = ctx.enter_context(tc.psum_pool(name="ps_h", bufs=4))
         ps_y = ctx.enter_context(tc.psum_pool(name="ps_y", bufs=1))
-        ps_misc = ctx.enter_context(tc.psum_pool(name="ps_misc", bufs=3))
+        ps_misc = ctx.enter_context(tc.psum_pool(name="ps_misc", bufs=2))
 
+        ident_f32 = const.tile([P, P], F32)
+        nc.vector.memset(ident_f32[:], 0.0)
+        make_identity(nc, ident_f32[:], nomemset=True)
+        b2_rows = const.tile([P, E * D], BF16)
+        nc.vector.memset(b2_rows[:], 0.0)
+        ones = const.tile([P, P], BF16)
+        nc.vector.memset(ones[:], 1.0)
+        warm = const.tile([P, 1], F32)
+        nc.vector.memset(warm[:], 0.0)
+        ident_bf = const.tile([P, P], BF16)
+        nc.vector.tensor_copy(out=ident_bf[:], in_=ident_f32[:])
+
+        nc.scalar.dma_start(out=b2_rows[0:1, :], in_=b2.rearrange("(o e) d -> o (e d)", o=1))
+        nc.scalar.activation(out=warm[:], in_=warm[:], func=ACT.Exp)
         phi_sb = loads.tile([P, E, D], BF16)
         nc.sync.dma_start(out=phi_sb[:], in_=phi.rearrange("e s d -> s e d"))
         x_sb = loads.tile([P, B, D], BF16)
         nc.sync.dma_start(out=x_sb[:], in_=x.rearrange("b n d -> n b d"))
-        bias_sb = loads.tile([P, E * D], BF16)
-        nc.gpsimd.dma_start(out=bias_sb[:], in_=b2.rearrange("e d -> (e d)").partition_broadcast(P))
         w2_raw = []
         h_sb = []
         for e in range(E):
-            raw = loads.tile([P, PASSES, PACK, D], BF16, name="w2_raw_%d" % e)
-            nc.sync.dma_start(
-                out=raw[:].rearrange("q g (u c) d -> q (g u) (c d)", c=2),
-                in_=w2[e].rearrange("(j q c) d -> q j (c d)", q=P, c=2),
-            )
-            w2_raw.append(raw)
             for b in range(B):
                 rows = loads.tile([P, H], BF16, name="h_sb_%d_%d" % (b, e))
                 nc.sync.dma_start(out=rows[:], in_=h[b, e])
                 h_sb.append(rows)
+                if b == 0:
+                    raw = loads.tile([P, PASSES, PACK, D], BF16, name="w2_raw_%d" % e)
+                    nc.sync.dma_start(
+                        out=raw[:].rearrange("q g (u c) d -> q (g u) (c d)", c=2),
+                        in_=w2[e].rearrange("(j q c) d -> q j (c d)", q=P, c=2),
+                    )
+                    w2_raw.append(raw)
 
-        ident_bf = const.tile([P, P], BF16)
-        make_identity(nc, ident_bf[:])
-        ident_f32 = const.tile([P, P], F32)
-        make_identity(nc, ident_f32[:])
-        warm = const.tile([P, 1], F32)
-        nc.vector.memset(warm[:], 0.0)
-        nc.scalar.activation(out=warm[:], in_=warm[:], func=ACT.Exp)
+        w2_grouped = [
+            work.tile([P, PASSES, D, PACK], BF16, name="w2_grouped_%d" % e, align_bytes=64) for e in range(E)
+        ]
+        w2_codes = [work.tile([P, PASSES, D], U32, name="w2_codes_%d" % e, align_bytes=64) for e in range(E)]
+        w2_scales = [work.tile([P, PASSES, D], U8, name="w2_scales_%d" % e, align_bytes=64) for e in range(E)]
+        h_grouped = [
+            work.tile([P, PASSES * S * PACK], BF16, name="h_grouped_%d" % i, align_bytes=64) for i in range(E * B)
+        ]
+        h_codes = [work.tile([P, PASSES, S], U32, name="h_codes_%d" % i, align_bytes=64) for i in range(E * B)]
+        h_scales = [work.tile([P, PASSES, S], U8, name="h_scales_%d" % i, align_bytes=64) for i in range(E * B)]
+        y_ps = [ps_y.tile([P, E, D], F32, name="y_ps_%d" % b) for b in range(B)]
+        p_sb = [work.tile([P, E, S], BF16, name="p_sb_%d" % b) for b in range(B)]
+        p_codes = [work.tile([P, N], U32, name="p_codes_%d" % b, align_bytes=64) for b in range(B)]
+        p_scales = [work.tile([P, N], U8, name="p_scales_%d" % b, align_bytes=64) for b in range(B)]
+        p_sum = [work.tile([P, 1], F32, name="p_sum_%d" % b) for b in range(B)]
+        inv_sum = [work.tile([P, 1], F32, name="inv_sum_%d" % b) for b in range(B)]
 
-        xphi_ps = ps_misc.tile([P, B + E, P], BF16, tag="misc")
-        for b in range(B):
-            nc.tensor.transpose(xphi_ps[:, b, :], x_sb[:, b, :], ident_bf[:])
-        for e in range(E):
-            nc.tensor.transpose(xphi_ps[:, B + e, :], phi_sb[:, e, :], ident_bf[:])
-        xphi_t = work.tile([P, B + E, P], BF16)
-        nc.vector.tensor_copy(out=xphi_t[:], in_=xphi_ps[:])
+        def regroup_w2(e):
+            nc.vector.tensor_copy(out=w2_grouped[e][:], in_=w2_raw[e][:].rearrange("q g t d -> q g d t"))
 
-        p_codes = []
-        p_scales = []
-        inv_sum = []
-        for b in range(B):
-            logits = ps_misc.tile([P, E * S], F32, tag="misc", name="logits_%d" % b)
-            nc.tensor.matmul(
-                out=logits[:],
-                lhsT=xphi_t[:, b, :],
-                rhs=xphi_t[:, B:, :].rearrange("d e s -> d (e s)"),
-                start=True,
-                stop=True,
-            )
-            neg_max = work.tile([P, 1], F32, name="neg_max_%d" % b)
-            nc.vector.tensor_reduce(
-                out=neg_max[:], in_=logits[:], axis=mybir.AxisListType.X, op=ALU.max, negate=True
-            )
-            p_sb = work.tile([P, E, S], BF16, name="p_sb_%d" % b)
-            p_sum = work.tile([P, 1], F32, name="p_sum_%d" % b)
-            nc.scalar.activation(
-                out=p_sb[:].rearrange("n e s -> n (e s)"),
-                in_=logits[:],
-                func=ACT.Exp,
-                bias=neg_max[:],
-                scale=1.0,
-                accum_out=p_sum[:],
-            )
-            inv = work.tile([P, 1], F32, name="inv_sum_%d" % b)
-            nc.vector.reciprocal(out=inv[:], in_=p_sum[:])
-            inv_sum.append(inv)
-
-            p_ps = ps_misc.tile([P, E, N], BF16, tag="misc", name="p_ps_%d" % b)
-            for e in range(E):
-                nc.tensor.transpose(p_ps[:, e, :], p_sb[:, e, :], ident_bf[:])
-            p_grouped = work.tile([P, N, PACK], BF16, name="p_grouped_%d" % b, align_bytes=64)
-            nc.vector.tensor_copy(out=p_grouped[:], in_=p_ps[:].rearrange("s e n -> s n e"))
-            codes = work.tile([P, N], U32, name="p_codes_%d" % b, align_bytes=64)
-            scales = work.tile([P, N], U8, name="p_scales_%d" % b, align_bytes=64)
+        def quantise_w2(e):
             nc.vector.quantize_mx(
-                out=codes[:].bitcast(FP8X4),
-                scales=scales[:],
-                in_=p_grouped[:].rearrange("s n e -> s (n e)"),
+                out=w2_codes[e][:].rearrange("q g d -> q (g d)").bitcast(FP8X4),
+                scales=w2_scales[e][:].rearrange("q g d -> q (g d)"),
+                in_=w2_grouped[e][:].rearrange("q g d t -> q (g d t)"),
             )
-            p_codes.append(codes)
-            p_scales.append(scales)
 
-        y_ps = []
-        for b in range(B):
-            y_ps.append(ps_y.tile([P, E, D], F32, name="y_ps_%d" % b))
-        for e in range(E):
-            w2_grouped = work.tile([P, PASSES, D, PACK], BF16, name="w2_grouped_%d" % e, align_bytes=64)
-            nc.vector.tensor_copy(out=w2_grouped[:], in_=w2_raw[e][:].rearrange("q g t d -> q g d t"))
-            w2_codes = work.tile([P, PASSES, D], U32, name="w2_codes_%d" % e, align_bytes=64)
-            w2_scales = work.tile([P, PASSES, D], U8, name="w2_scales_%d" % e, align_bytes=64)
-            nc.vector.quantize_mx(
-                out=w2_codes[:].rearrange("q g d -> q (g d)").bitcast(FP8X4),
-                scales=w2_scales[:].rearrange("q g d -> q (g d)"),
-                in_=w2_grouped[:].rearrange("q g d t -> q (g d t)"),
+        def transpose_h(b, e):
+            words = h_sb[e * B + b][:].bitcast(F32)
+            h_ps = ps_h.tile([P, PASSES * HALVES, S], F32, tag="h_ps")
+            for j in range(PASSES * HALVES):
+                nc.tensor.transpose(h_ps[:, j, :], words[:, j * P : (j + 1) * P], ident_f32[:])
+            nc.scalar.copy(
+                out=h_grouped[e * B + b][:].bitcast(F32).rearrange("q (g s u) -> q g s u", g=PASSES, u=HALVES),
+                in_=h_ps[:].rearrange("q (g u) s -> q g s u", u=HALVES),
             )
+
+        def quantise_h(b, e):
+            nc.vector.quantize_mx(
+                out=h_codes[e * B + b][:].rearrange("q g s -> q (g s)").bitcast(FP8X4),
+                scales=h_scales[e * B + b][:].rearrange("q g s -> q (g s)"),
+                in_=h_grouped[e * B + b][:],
+            )
+
+        def second_layer(e):
             for b in range(B):
-                words = h_sb[e * B + b][:].bitcast(F32)
-                h_ps = ps_h.tile([P, PASSES * HALVES, S], F32, tag="h_ps")
-                for j in range(PASSES * HALVES):
-                    nc.tensor.transpose(h_ps[:, j, :], words[:, j * P : (j + 1) * P], ident_f32[:])
-                h_grouped = work.tile([P, PASSES * S * PACK], BF16, name="h_grouped_%d_%d" % (b, e), align_bytes=64)
-                nc.scalar.copy(
-                    out=h_grouped[:].bitcast(F32).rearrange("q (g s u) -> q g s u", g=PASSES, u=HALVES),
-                    in_=h_ps[:].rearrange("q (g u) s -> q g s u", u=HALVES),
-                )
-                h_codes = work.tile([P, PASSES, S], U32, name="h_codes_%d_%d" % (b, e), align_bytes=64)
-                h_scales = work.tile([P, PASSES, S], U8, name="h_scales_%d_%d" % (b, e), align_bytes=64)
-                nc.vector.quantize_mx(
-                    out=h_codes[:].rearrange("q g s -> q (g s)").bitcast(FP8X4),
-                    scales=h_scales[:].rearrange("q g s -> q (g s)"),
-                    in_=h_grouped[:],
-                )
                 for g in range(PASSES):
                     nc.tensor.matmul_mx(
                         out=y_ps[b][:, e, :],
-                        lhsT=h_codes[:, g, :].bitcast(FP8X4),
-                        lhsT_scale=h_scales[:, g, :],
-                        rhs=w2_codes[:, g, :].bitcast(FP8X4),
-                        rhs_scale=w2_scales[:, g, :],
+                        lhsT=h_codes[e * B + b][:, g, :].bitcast(FP8X4),
+                        lhsT_scale=h_scales[e * B + b][:, g, :],
+                        rhs=w2_codes[e][:, g, :].bitcast(FP8X4),
+                        rhs_scale=w2_scales[e][:, g, :],
                         start=(g == 0),
                         stop=(g == PASSES - 1),
                     )
 
+        def softmax_numerators():
+            for b in range(B):
+                logits = ps_misc.tile([P, E * S], F32, tag="misc", name="logits_%d" % b)
+                nc.tensor.matmul(
+                    out=logits[:],
+                    lhsT=xphi_t[:, b, :],
+                    rhs=xphi_t[:, B:, :].rearrange("d e s -> d (e s)"),
+                    start=True,
+                    stop=True,
+                )
+                neg_max = work.tile([P, 1], F32, name="neg_max_%d" % b)
+                nc.vector.tensor_reduce(
+                    out=neg_max[:], in_=logits[:], axis=mybir.AxisListType.X, op=ALU.max, negate=True
+                )
+                nc.scalar.activation(
+                    out=p_sb[b][:].rearrange("n e s -> n (e s)"),
+                    in_=logits[:],
+                    func=ACT.Exp,
+                    bias=neg_max[:],
+                    scale=1.0,
+                    accum_out=p_sum[b][:],
+                )
+
+        def quantise_p():
+            p_grouped = []
+            for b in range(B):
+                p_ps = ps_misc.tile([P, E, N], BF16, tag="misc", name="p_ps_%d" % b)
+                for e in range(E):
+                    nc.tensor.transpose(p_ps[:, e, :], p_sb[b][:, e, :], ident_bf[:])
+                grouped = work.tile([P, N, PACK], BF16, name="p_grouped_%d" % b, align_bytes=64)
+                nc.scalar.copy(out=grouped[:], in_=p_ps[:].rearrange("s e n -> s n e"))
+                p_grouped.append(grouped)
+            for b in range(B):
+                nc.vector.reciprocal(out=inv_sum[b][:], in_=p_sum[b][:])
+                nc.vector.quantize_mx(
+                    out=p_codes[b][:].bitcast(FP8X4),
+                    scales=p_scales[b][:],
+                    in_=p_grouped[b][:].rearrange("s n e -> s (n e)"),
+                )
+
+        xphi_ps = ps_misc.tile([P, B + E, P], BF16, tag="misc")
+        for e in range(E):
+            nc.tensor.transpose(xphi_ps[:, B + e, :], phi_sb[:, e, :], ident_bf[:])
         for b in range(B):
-            y_grouped = work.tile([P, D, PACK], BF16, name="y_grouped_%d" % b, align_bytes=64)
+            nc.tensor.transpose(xphi_ps[:, b, :], x_sb[:, b, :], ident_bf[:])
+        xphi_t = work.tile([P, B + E, P], BF16)
+        nc.scalar.copy(out=xphi_t[:], in_=xphi_ps[:])
+        bias_ps = ps_misc.tile([P, E * D], BF16, tag="misc")
+        nc.tensor.matmul(out=bias_ps[:], lhsT=ones[:], rhs=b2_rows[:], start=True, stop=True)
+        bias_sb = work.tile([P, E * D], BF16)
+        nc.scalar.copy(out=bias_sb[:], in_=bias_ps[:])
+
+        regroup_w2(0)
+        for e in range(E):
+            transpose_h(0, e)
+            transpose_h(1, e)
+            if e > 0:
+                second_layer(e - 1)
+            quantise_w2(e)
+            quantise_h(0, e)
+            if e + 1 < E:
+                regroup_w2(e + 1)
+            quantise_h(1, e)
+            if e == LOGITS_ROUND:
+                softmax_numerators()
+            if e == P_ROUND:
+                quantise_p()
+        second_layer(E - 1)
+
+        y_grouped = [work.tile([P, D, PACK], BF16, name="y_grouped_%d" % b, align_bytes=64) for b in range(B)]
+        for b in range(B):
             nc.vector.tensor_tensor(
-                out=y_grouped[:],
+                out=y_grouped[b][:],
                 in0=y_ps[b][:].rearrange("s e d -> s d e"),
                 in1=bias_sb[:].rearrange("s (e d) -> s d e", e=E),
                 op=ALU.add,
             )
+        for b in range(B):
             y_codes = work.tile([P, D], U32, name="y_codes_%d" % b, align_bytes=64)
             y_scales = work.tile([P, D], U8, name="y_scales_%d" % b, align_bytes=64)
             nc.vector.quantize_mx(
                 out=y_codes[:].bitcast(FP8X4),
                 scales=y_scales[:],
-                in_=y_grouped[:].rearrange("s d e -> s (d e)"),
+                in_=y_grouped[b][:].rearrange("s d e -> s (d e)"),
             )
             o_ps = ps_misc.tile([P, D], F32, tag="misc", name="o_ps_%d" % b)
             nc.tensor.matmul_mx(
@@ -179,7 +220,5 @@ def tile_mixtureexpertsmlp_pb_s_kernel(tc, h, w2, b2, x, phi, out):
                 stop=True,
             )
             o_sb = work.tile([P, D], F32, name="o_sb_%d" % b)
-            nc.vector.tensor_scalar(
-                out=o_sb[:], in0=o_ps[:], scalar1=inv_sum[b][:], scalar2=None, op0=ALU.mult
-            )
+            nc.scalar.activation(out=o_sb[:], in_=o_ps[:], func=ACT.Copy, scale=inv_sum[b][:])
             nc.sync.dma_start(out=out[b], in_=o_sb[:])

@@ -17,8 +17,7 @@ PACK = 4
 K_PASS = P * PACK
 PASSES = H // K_PASS
 HALVES = 2
-LOGITS_ROUND = 0
-P_ROUND = 1
+QUANTISE_LAG = 2
 
 FLOPS = 2 * (B * E * S * H * D + B * N * D * E * S + B * N * E * S * D)
 
@@ -79,6 +78,7 @@ def tile_mixtureexpertsmlp_pb_s_kernel(tc, h, w2, b2, x, phi, out):
         h_scales = [work.tile([P, PASSES, S], U8, name="h_scales_%d" % i, align_bytes=64) for i in range(E * B)]
         y_ps = [ps_y.tile([P, E, D], F32, name="y_ps_%d" % b) for b in range(B)]
         p_sb = [work.tile([P, E, S], BF16, name="p_sb_%d" % b) for b in range(B)]
+        p_grouped = [work.tile([P, N, PACK], BF16, name="p_grouped_%d" % b, align_bytes=64) for b in range(B)]
         p_codes = [work.tile([P, N], U32, name="p_codes_%d" % b, align_bytes=64) for b in range(B)]
         p_scales = [work.tile([P, N], U8, name="p_scales_%d" % b, align_bytes=64) for b in range(B)]
         p_sum = [work.tile([P, 1], F32, name="p_sum_%d" % b) for b in range(B)]
@@ -124,46 +124,46 @@ def tile_mixtureexpertsmlp_pb_s_kernel(tc, h, w2, b2, x, phi, out):
                         stop=(g == PASSES - 1),
                     )
 
-        def softmax_numerators():
-            for b in range(B):
-                logits = ps_misc.tile([P, E * S], F32, tag="misc", name="logits_%d" % b)
-                nc.tensor.matmul(
-                    out=logits[:],
-                    lhsT=xphi_t[:, b, :],
-                    rhs=xphi_t[:, B:, :].rearrange("d e s -> d (e s)"),
-                    start=True,
-                    stop=True,
-                )
-                neg_max = work.tile([P, 1], F32, name="neg_max_%d" % b)
-                nc.vector.tensor_reduce(
-                    out=neg_max[:], in_=logits[:], axis=mybir.AxisListType.X, op=ALU.max, negate=True
-                )
-                nc.scalar.activation(
-                    out=p_sb[b][:].rearrange("n e s -> n (e s)"),
-                    in_=logits[:],
-                    func=ACT.Exp,
-                    bias=neg_max[:],
-                    scale=1.0,
-                    accum_out=p_sum[b][:],
-                )
+        def softmax_numerators(b):
+            logits = ps_misc.tile([P, E * S], F32, tag="misc", name="logits_%d" % b)
+            nc.tensor.matmul(
+                out=logits[:],
+                lhsT=xphi_t[:, b, :],
+                rhs=xphi_t[:, B:, :].rearrange("d e s -> d (e s)"),
+                start=True,
+                stop=True,
+            )
+            neg_max = work.tile([P, 1], F32, name="neg_max_%d" % b)
+            nc.vector.tensor_reduce(
+                out=neg_max[:], in_=logits[:], axis=mybir.AxisListType.X, op=ALU.max, negate=True
+            )
+            nc.scalar.activation(
+                out=p_sb[b][:].rearrange("n e s -> n (e s)"),
+                in_=logits[:],
+                func=ACT.Exp,
+                bias=neg_max[:],
+                scale=1.0,
+                accum_out=p_sum[b][:],
+            )
 
-        def quantise_p():
-            p_grouped = []
-            for b in range(B):
-                p_ps = ps_misc.tile([P, E, N], BF16, tag="misc", name="p_ps_%d" % b)
-                for e in range(E):
-                    nc.tensor.transpose(p_ps[:, e, :], p_sb[b][:, e, :], ident_bf[:])
-                grouped = work.tile([P, N, PACK], BF16, name="p_grouped_%d" % b, align_bytes=64)
-                nc.scalar.copy(out=grouped[:], in_=p_ps[:].rearrange("s e n -> s n e"))
-                p_grouped.append(grouped)
-            for b in range(B):
-                nc.vector.reciprocal(out=inv_sum[b][:], in_=p_sum[b][:])
-                nc.vector.quantize_mx(
-                    out=p_codes[b][:].bitcast(FP8X4),
-                    scales=p_scales[b][:],
-                    in_=p_grouped[b][:].rearrange("s n e -> s (n e)"),
-                )
+        def transpose_p(b):
+            p_ps = ps_misc.tile([P, E, N], BF16, tag="misc", name="p_ps_%d" % b)
+            for e in range(E):
+                nc.tensor.transpose(p_ps[:, e, :], p_sb[b][:, e, :], ident_bf[:])
+            nc.scalar.copy(out=p_grouped[b][:], in_=p_ps[:].rearrange("s e n -> s n e"))
 
+        def quantise_p(b):
+            nc.vector.reciprocal(out=inv_sum[b][:], in_=p_sum[b][:])
+            nc.vector.quantize_mx(
+                out=p_codes[b][:].bitcast(FP8X4),
+                scales=p_scales[b][:],
+                in_=p_grouped[b][:].rearrange("s n e -> s (n e)"),
+            )
+
+        bias_ps = ps_misc.tile([P, E * D], BF16, tag="misc")
+        nc.tensor.matmul(out=bias_ps[:], lhsT=ones[:], rhs=b2_rows[:], start=True, stop=True)
+        bias_sb = work.tile([P, E * D], BF16)
+        nc.scalar.copy(out=bias_sb[:], in_=bias_ps[:])
         xphi_ps = ps_misc.tile([P, B + E, P], BF16, tag="misc")
         for e in range(E):
             nc.tensor.transpose(xphi_ps[:, B + e, :], phi_sb[:, e, :], ident_bf[:])
@@ -171,26 +171,27 @@ def tile_mixtureexpertsmlp_pb_s_kernel(tc, h, w2, b2, x, phi, out):
             nc.tensor.transpose(xphi_ps[:, b, :], x_sb[:, b, :], ident_bf[:])
         xphi_t = work.tile([P, B + E, P], BF16)
         nc.scalar.copy(out=xphi_t[:], in_=xphi_ps[:])
-        bias_ps = ps_misc.tile([P, E * D], BF16, tag="misc")
-        nc.tensor.matmul(out=bias_ps[:], lhsT=ones[:], rhs=b2_rows[:], start=True, stop=True)
-        bias_sb = work.tile([P, E * D], BF16)
-        nc.scalar.copy(out=bias_sb[:], in_=bias_ps[:])
 
-        regroup_w2(0)
-        for e in range(E):
-            transpose_h(0, e)
-            transpose_h(1, e)
-            if e > 0:
+        blocks = [(b, e) for e in range(E) for b in range(B)]
+        for step in range(len(blocks)):
+            b, e = blocks[step]
+            transpose_h(b, e)
+            if b == B - 1:
+                regroup_w2(e)
+            if e == 0:
+                softmax_numerators(b)
+            if e == 1:
+                transpose_p(b)
+            if step >= QUANTISE_LAG:
+                quantise_h(*blocks[step - QUANTISE_LAG])
+            if b == B - 1:
+                quantise_w2(e)
+            if e == 2:
+                quantise_p(b)
+            if b == B - 1 and e > 0:
                 second_layer(e - 1)
-            quantise_w2(e)
-            quantise_h(0, e)
-            if e + 1 < E:
-                regroup_w2(e + 1)
-            quantise_h(1, e)
-            if e == LOGITS_ROUND:
-                softmax_numerators()
-            if e == P_ROUND:
-                quantise_p()
+        for block in blocks[len(blocks) - QUANTISE_LAG :]:
+            quantise_h(*block)
         second_layer(E - 1)
 
         y_grouped = [work.tile([P, D, PACK], BF16, name="y_grouped_%d" % b, align_bytes=64) for b in range(B)]

@@ -81,6 +81,7 @@ def tile_mixtureexpertsmlp_pb_s_kernel(tc, h, w2, b2, x, phi, out):
         p_grouped = [work.tile([P, N, PACK], BF16, name="p_grouped_%d" % b, align_bytes=64) for b in range(B)]
         p_codes = [work.tile([P, N], U32, name="p_codes_%d" % b, align_bytes=64) for b in range(B)]
         p_scales = [work.tile([P, N], U8, name="p_scales_%d" % b, align_bytes=64) for b in range(B)]
+        bias_sb = work.tile([P, E * D], BF16)
         p_sum = [work.tile([P, 1], F32, name="p_sum_%d" % b) for b in range(B)]
         inv_sum = [work.tile([P, 1], F32, name="inv_sum_%d" % b) for b in range(B)]
 
@@ -146,6 +147,11 @@ def tile_mixtureexpertsmlp_pb_s_kernel(tc, h, w2, b2, x, phi, out):
                 accum_out=p_sum[b][:],
             )
 
+        def spread_bias():
+            bias_ps = ps_misc.tile([P, E * D], BF16, tag="misc")
+            nc.tensor.matmul(out=bias_ps[:], lhsT=ones[:], rhs=b2_rows[:], start=True, stop=True)
+            nc.scalar.copy(out=bias_sb[:], in_=bias_ps[:])
+
         def transpose_p(b):
             p_ps = ps_misc.tile([P, E, N], BF16, tag="misc", name="p_ps_%d" % b)
             for e in range(E):
@@ -160,10 +166,6 @@ def tile_mixtureexpertsmlp_pb_s_kernel(tc, h, w2, b2, x, phi, out):
                 in_=p_grouped[b][:].rearrange("s n e -> s (n e)"),
             )
 
-        bias_ps = ps_misc.tile([P, E * D], BF16, tag="misc")
-        nc.tensor.matmul(out=bias_ps[:], lhsT=ones[:], rhs=b2_rows[:], start=True, stop=True)
-        bias_sb = work.tile([P, E * D], BF16)
-        nc.scalar.copy(out=bias_sb[:], in_=bias_ps[:])
         xphi_ps = ps_misc.tile([P, B + E, P], BF16, tag="misc")
         for e in range(E):
             nc.tensor.transpose(xphi_ps[:, B + e, :], phi_sb[:, e, :], ident_bf[:])
@@ -190,6 +192,8 @@ def tile_mixtureexpertsmlp_pb_s_kernel(tc, h, w2, b2, x, phi, out):
                 quantise_p(b)
             if b == B - 1 and e > 0:
                 second_layer(e - 1)
+            if b == B - 1 and e == 2:
+                spread_bias()
         for block in blocks[len(blocks) - QUANTISE_LAG :]:
             quantise_h(*block)
         second_layer(E - 1)

@@ -17,7 +17,6 @@ PACK = 4
 K_PASS = P * PACK
 PASSES = H // K_PASS
 HALVES = 2
-QUANTISE_LAG = 2
 
 FLOPS = 2 * (B * E * S * H * D + B * N * D * E * S + B * N * E * S * D)
 
@@ -33,49 +32,66 @@ def tile_mixtureexpertsmlp_pb_s_kernel(tc, h, w2, b2, x, phi, out):
         ps_y = ctx.enter_context(tc.psum_pool(name="ps_y", bufs=1))
         ps_misc = ctx.enter_context(tc.psum_pool(name="ps_misc", bufs=2))
 
+        b2_rows = const.tile([P, E * D], BF16)
+        nc.vector.memset(b2_rows[:].bitcast(U32), 0)
+        nc.scalar.dma_start(out=b2_rows[0:1, :], in_=b2.rearrange("(o e) d -> o (e d)", o=1))
+        warm = const.tile([P, 1], F32)
+        nc.vector.memset(warm[:], 0.0)
+        nc.scalar.activation(out=warm[:], in_=warm[:], func=ACT.Exp)
         ident_f32 = const.tile([P, P], F32)
         nc.vector.memset(ident_f32[:], 0.0)
         make_identity(nc, ident_f32[:], nomemset=True)
-        b2_rows = const.tile([P, E * D], BF16)
-        nc.vector.memset(b2_rows[:], 0.0)
         ones = const.tile([P, P], BF16)
         nc.vector.memset(ones[:], 1.0)
-        warm = const.tile([P, 1], F32)
-        nc.vector.memset(warm[:], 0.0)
         ident_bf = const.tile([P, P], BF16)
         nc.vector.tensor_copy(out=ident_bf[:], in_=ident_f32[:])
 
-        nc.scalar.dma_start(out=b2_rows[0:1, :], in_=b2.rearrange("(o e) d -> o (e d)", o=1))
-        nc.scalar.activation(out=warm[:], in_=warm[:], func=ACT.Exp)
+        w2_raw = {}
+        h_sb = {}
         phi_sb = loads.tile([P, E, D], BF16)
-        nc.sync.dma_start(out=phi_sb[:], in_=phi.rearrange("e s d -> s e d"))
         x_sb = loads.tile([P, B, D], BF16)
-        nc.sync.dma_start(out=x_sb[:], in_=x.rearrange("b n d -> n b d"))
-        w2_raw = []
-        h_sb = []
-        for e in range(E):
-            for b in range(B):
-                rows = loads.tile([P, H], BF16, name="h_sb_%d_%d" % (b, e))
-                nc.sync.dma_start(out=rows[:], in_=h[b, e])
-                h_sb.append(rows)
-                if b == 0:
-                    raw = loads.tile([P, PASSES, PACK, D], BF16, name="w2_raw_%d" % e)
-                    nc.sync.dma_start(
-                        out=raw[:].rearrange("q g (u c) d -> q (g u) (c d)", c=2),
-                        in_=w2[e].rearrange("(j q c) d -> q j (c d)", q=P, c=2),
-                    )
-                    w2_raw.append(raw)
+
+        def load_w2(e):
+            raw = loads.tile([P, PASSES, PACK, D], BF16, name="w2_raw_%d" % e)
+            nc.sync.dma_start(
+                out=raw[:].rearrange("q g (u c) d -> q (g u) (c d)", c=2),
+                in_=w2[e].rearrange("(j q c) d -> q j (c d)", q=P, c=2),
+            )
+            w2_raw[e] = raw
+
+        def load_h(b, e):
+            rows = loads.tile([P, H], BF16, name="h_sb_%d_%d" % (b, e))
+            nc.sync.dma_start(out=rows[:], in_=h[b, e])
+            h_sb[b, e] = rows
+
+        nc.sync.dma_start(out=phi_sb[:], in_=phi.rearrange("e s d -> (e s) d").rearrange("(q j) d -> q j d", j=E))
+        nc.sync.dma_start(out=x_sb[:], in_=x.rearrange("b n d -> (b n) d").rearrange("(q j) d -> q j d", j=B))
+        load_h(0, 0)
+        load_h(1, 0)
+        load_w2(0)
+        load_h(0, 1)
+        load_w2(1)
+        load_h(1, 1)
+        load_w2(2)
+        load_h(0, 2)
+        load_w2(3)
+        load_h(0, 3)
+        load_h(1, 2)
+        load_h(1, 3)
 
         w2_grouped = [
             work.tile([P, PASSES, D, PACK], BF16, name="w2_grouped_%d" % e, align_bytes=64) for e in range(E)
         ]
         w2_codes = [work.tile([P, PASSES, D], U32, name="w2_codes_%d" % e, align_bytes=64) for e in range(E)]
         w2_scales = [work.tile([P, PASSES, D], U8, name="w2_scales_%d" % e, align_bytes=64) for e in range(E)]
-        h_grouped = [
-            work.tile([P, PASSES * S * PACK], BF16, name="h_grouped_%d" % i, align_bytes=64) for i in range(E * B)
-        ]
-        h_codes = [work.tile([P, PASSES, S], U32, name="h_codes_%d" % i, align_bytes=64) for i in range(E * B)]
-        h_scales = [work.tile([P, PASSES, S], U8, name="h_scales_%d" % i, align_bytes=64) for i in range(E * B)]
+        blocks = [(b, e) for b in range(B) for e in range(E)]
+        h_grouped = {}
+        h_codes = {}
+        h_scales = {}
+        for b, e in blocks:
+            h_grouped[b, e] = work.tile([P, PASSES * S * PACK], BF16, name="h_grouped_%d_%d" % (b, e), align_bytes=64)
+            h_codes[b, e] = work.tile([P, PASSES, S], U32, name="h_codes_%d_%d" % (b, e), align_bytes=64)
+            h_scales[b, e] = work.tile([P, PASSES, S], U8, name="h_scales_%d_%d" % (b, e), align_bytes=64)
         y_ps = [ps_y.tile([P, E, D], F32, name="y_ps_%d" % b) for b in range(B)]
         p_sb = [work.tile([P, E, S], BF16, name="p_sb_%d" % b) for b in range(B)]
         p_grouped = [work.tile([P, N, PACK], BF16, name="p_grouped_%d" % b, align_bytes=64) for b in range(B)]
@@ -84,48 +100,103 @@ def tile_mixtureexpertsmlp_pb_s_kernel(tc, h, w2, b2, x, phi, out):
         bias_sb = work.tile([P, E * D], BF16)
         p_sum = [work.tile([P, 1], F32, name="p_sum_%d" % b) for b in range(B)]
         inv_sum = [work.tile([P, 1], F32, name="inv_sum_%d" % b) for b in range(B)]
+        y_grouped = [work.tile([P, D, PACK], BF16, name="y_grouped_%d" % b, align_bytes=64) for b in range(B)]
+        y_codes = [work.tile([P, D], U32, name="y_codes_%d" % b, align_bytes=64) for b in range(B)]
+        y_scales = [work.tile([P, D], U8, name="y_scales_%d" % b, align_bytes=64) for b in range(B)]
+        o_sb = [work.tile([P, D], F32, name="o_sb_%d" % b) for b in range(B)]
 
-        def regroup_w2(e):
+        h_banks = {}
+        misc = {}
+
+        def rg(e):
             nc.vector.tensor_copy(out=w2_grouped[e][:], in_=w2_raw[e][:].rearrange("q g t d -> q g d t"))
 
-        def quantise_w2(e):
+        def rgP(e):
+            nc.gpsimd.tensor_scalar(
+                out=w2_grouped[e][:], in0=w2_raw[e][:].rearrange("q g t d -> q g d t"),
+                scalar1=1.0, scalar2=0.0, op0=ALU.mult, op1=ALU.add,
+            )
+
+        def rgA(e):
+            nc.scalar.copy(out=w2_grouped[e][:], in_=w2_raw[e][:].rearrange("q g t d -> q g d t"))
+
+        def qw(e):
             nc.vector.quantize_mx(
                 out=w2_codes[e][:].rearrange("q g d -> q (g d)").bitcast(FP8X4),
                 scales=w2_scales[e][:].rearrange("q g d -> q (g d)"),
                 in_=w2_grouped[e][:].rearrange("q g d t -> q (g d t)"),
             )
 
-        def transpose_h(b, e):
-            words = h_sb[e * B + b][:].bitcast(F32)
+        def T(b, e):
+            words = h_sb[b, e][:].bitcast(F32)
             h_ps = ps_h.tile([P, PASSES * HALVES, S], F32, tag="h_ps")
             for j in range(PASSES * HALVES):
                 nc.tensor.transpose(h_ps[:, j, :], words[:, j * P : (j + 1) * P], ident_f32[:])
+            h_banks[b, e] = h_ps
+
+        def c(b, e):
             nc.scalar.copy(
-                out=h_grouped[e * B + b][:].bitcast(F32).rearrange("q (g s u) -> q g s u", g=PASSES, u=HALVES),
-                in_=h_ps[:].rearrange("q (g u) s -> q g s u", u=HALVES),
+                out=h_grouped[b, e][:].bitcast(F32).rearrange("q (g s u) -> q g s u", g=PASSES, u=HALVES),
+                in_=h_banks[b, e][:].rearrange("q (g u) s -> q g s u", u=HALVES),
             )
 
-        def quantise_h(b, e):
+        def cV(b, e):
+            nc.vector.tensor_copy(
+                out=h_grouped[b, e][:].bitcast(F32).rearrange("q (g s u) -> q g s u", g=PASSES, u=HALVES),
+                in_=h_banks[b, e][:].rearrange("q (g u) s -> q g s u", u=HALVES),
+            )
+
+        def q(b, e):
             nc.vector.quantize_mx(
-                out=h_codes[e * B + b][:].rearrange("q g s -> q (g s)").bitcast(FP8X4),
-                scales=h_scales[e * B + b][:].rearrange("q g s -> q (g s)"),
-                in_=h_grouped[e * B + b][:],
+                out=h_codes[b, e][:].rearrange("q g s -> q (g s)").bitcast(FP8X4),
+                scales=h_scales[b, e][:].rearrange("q g s -> q (g s)"),
+                in_=h_grouped[b, e][:],
             )
 
-        def second_layer(e):
-            for b in range(B):
-                for g in range(PASSES):
-                    nc.tensor.matmul_mx(
-                        out=y_ps[b][:, e, :],
-                        lhsT=h_codes[e * B + b][:, g, :].bitcast(FP8X4),
-                        lhsT_scale=h_scales[e * B + b][:, g, :],
-                        rhs=w2_codes[e][:, g, :].bitcast(FP8X4),
-                        rhs_scale=w2_scales[e][:, g, :],
-                        start=(g == 0),
-                        stop=(g == PASSES - 1),
-                    )
+        def half_T(b, e, banks):
+            words = h_sb[b, e][:].bitcast(F32)
+            for g in range(PASSES):
+                for u in range(HALVES):
+                    j = g * HALVES + u
+                    nc.tensor.transpose(banks[g][:, u, :], words[:, j * P : (j + 1) * P], ident_f32[:])
 
-        def softmax_numerators(b):
+        def M(b, e):
+            for g in range(PASSES):
+                nc.tensor.matmul_mx(
+                    out=y_ps[b][:, e, :],
+                    lhsT=h_codes[b, e][:, g, :].bitcast(FP8X4),
+                    lhsT_scale=h_scales[b, e][:, g, :],
+                    rhs=w2_codes[e][:, g, :].bitcast(FP8X4),
+                    rhs_scale=w2_scales[e][:, g, :],
+                    start=(g == 0),
+                    stop=(g == PASSES - 1),
+                )
+
+        xphi_t = work.tile([P, B + E, P], BF16)
+        neg_max = [work.tile([P, 1], F32, name="neg_max_%d" % b) for b in range(B)]
+
+        def Tx():
+            xphi_ps = ps_misc.tile([P, B + E, P], BF16, tag="misc")
+            for e in range(E):
+                nc.tensor.transpose(xphi_ps[:, B + e, :], phi_sb[:, e, :], ident_bf[:])
+            for b in range(B):
+                nc.tensor.transpose(xphi_ps[:, b, :], x_sb[:, b, :], ident_bf[:])
+            misc["x"] = xphi_ps
+
+        def xc():
+            nc.scalar.copy(
+                out=xphi_t[:, 0:B, :].rearrange("d b (r j) -> d b r j", j=B),
+                in_=misc["x"][:, 0:B, :].rearrange("d j (b r) -> d b r j", b=B),
+            )
+            nc.scalar.copy(
+                out=xphi_t[:, B:, :].rearrange("d e (r j) -> d e r j", j=E),
+                in_=misc["x"][:, B:, :].rearrange("d j (e r) -> d e r j", e=E),
+            )
+
+        def xcV():
+            nc.vector.tensor_copy(out=xphi_t[:], in_=misc["x"][:])
+
+        def L(b):
             logits = ps_misc.tile([P, E * S], F32, tag="misc", name="logits_%d" % b)
             nc.tensor.matmul(
                 out=logits[:],
@@ -134,96 +205,156 @@ def tile_mixtureexpertsmlp_pb_s_kernel(tc, h, w2, b2, x, phi, out):
                 start=True,
                 stop=True,
             )
-            neg_max = work.tile([P, 1], F32, name="neg_max_%d" % b)
+            misc["l", b] = logits
+
+        def mx(b):
             nc.vector.tensor_reduce(
-                out=neg_max[:], in_=logits[:], axis=mybir.AxisListType.X, op=ALU.max, negate=True
+                out=neg_max[b][:], in_=misc["l", b][:], axis=mybir.AxisListType.X, op=ALU.max, negate=True
             )
+
+        def ex(b):
             nc.scalar.activation(
                 out=p_sb[b][:].rearrange("n e s -> n (e s)"),
-                in_=logits[:],
+                in_=misc["l", b][:],
                 func=ACT.Exp,
-                bias=neg_max[:],
+                bias=neg_max[b][:],
                 scale=1.0,
                 accum_out=p_sum[b][:],
             )
 
-        def spread_bias():
-            bias_ps = ps_misc.tile([P, E * D], BF16, tag="misc")
+        def Bm():
+            bias_ps = ps_h.tile([P, E * D], BF16, tag="h_ps", name="bias_ps")
             nc.tensor.matmul(out=bias_ps[:], lhsT=ones[:], rhs=b2_rows[:], start=True, stop=True)
-            nc.scalar.copy(out=bias_sb[:], in_=bias_ps[:])
+            misc["b"] = bias_ps
 
-        def transpose_p(b):
+        def bc():
+            nc.scalar.copy(out=bias_sb[:], in_=misc["b"][:])
+
+        def bcV():
+            nc.vector.tensor_copy(out=bias_sb[:], in_=misc["b"][:])
+
+        def Tp(b):
             p_ps = ps_misc.tile([P, E, N], BF16, tag="misc", name="p_ps_%d" % b)
             for e in range(E):
                 nc.tensor.transpose(p_ps[:, e, :], p_sb[b][:, e, :], ident_bf[:])
-            nc.scalar.copy(out=p_grouped[b][:], in_=p_ps[:].rearrange("s e n -> s n e"))
+            misc["p", b] = p_ps
 
-        def quantise_p(b):
+        def pc(b):
+            nc.scalar.copy(out=p_grouped[b][:], in_=misc["p", b][:].rearrange("s e n -> s n e"))
+
+        def pcV(b):
+            nc.vector.tensor_copy(out=p_grouped[b][:], in_=misc["p", b][:].rearrange("s e n -> s n e"))
+
+        def rc(b):
             nc.vector.reciprocal(out=inv_sum[b][:], in_=p_sum[b][:])
+
+        def qp(b):
             nc.vector.quantize_mx(
                 out=p_codes[b][:].bitcast(FP8X4),
                 scales=p_scales[b][:],
                 in_=p_grouped[b][:].rearrange("s n e -> s (n e)"),
             )
 
-        xphi_ps = ps_misc.tile([P, B + E, P], BF16, tag="misc")
-        for e in range(E):
-            nc.tensor.transpose(xphi_ps[:, B + e, :], phi_sb[:, e, :], ident_bf[:])
-        for b in range(B):
-            nc.tensor.transpose(xphi_ps[:, b, :], x_sb[:, b, :], ident_bf[:])
-        xphi_t = work.tile([P, B + E, P], BF16)
-        nc.scalar.copy(out=xphi_t[:], in_=xphi_ps[:])
-
-        blocks = [(b, e) for e in range(E) for b in range(B)]
-        for step in range(len(blocks)):
-            b, e = blocks[step]
-            transpose_h(b, e)
-            if b == B - 1:
-                regroup_w2(e)
-            if e == 0:
-                softmax_numerators(b)
-            if e == 1:
-                transpose_p(b)
-            if step >= QUANTISE_LAG:
-                quantise_h(*blocks[step - QUANTISE_LAG])
-            if b == B - 1:
-                quantise_w2(e)
-            if e == 2:
-                quantise_p(b)
-            if b == B - 1 and e > 0:
-                second_layer(e - 1)
-            if b == B - 1 and e == 2:
-                spread_bias()
-        for block in blocks[len(blocks) - QUANTISE_LAG :]:
-            quantise_h(*block)
-        second_layer(E - 1)
-
-        y_grouped = [work.tile([P, D, PACK], BF16, name="y_grouped_%d" % b, align_bytes=64) for b in range(B)]
-        for b in range(B):
+        def add(b):
             nc.vector.tensor_tensor(
                 out=y_grouped[b][:],
                 in0=y_ps[b][:].rearrange("s e d -> s d e"),
                 in1=bias_sb[:].rearrange("s (e d) -> s d e", e=E),
                 op=ALU.add,
             )
-        for b in range(B):
-            y_codes = work.tile([P, D], U32, name="y_codes_%d" % b, align_bytes=64)
-            y_scales = work.tile([P, D], U8, name="y_scales_%d" % b, align_bytes=64)
+
+        def qy(b):
             nc.vector.quantize_mx(
-                out=y_codes[:].bitcast(FP8X4),
-                scales=y_scales[:],
+                out=y_codes[b][:].bitcast(FP8X4),
+                scales=y_scales[b][:],
                 in_=y_grouped[b][:].rearrange("s d e -> s (d e)"),
             )
+
+        def C(b):
             o_ps = ps_misc.tile([P, D], F32, tag="misc", name="o_ps_%d" % b)
             nc.tensor.matmul_mx(
                 out=o_ps[:],
                 lhsT=p_codes[b][:].bitcast(FP8X4),
                 lhsT_scale=p_scales[b][:],
-                rhs=y_codes[:].bitcast(FP8X4),
-                rhs_scale=y_scales[:],
+                rhs=y_codes[b][:].bitcast(FP8X4),
+                rhs_scale=y_scales[b][:],
                 start=True,
                 stop=True,
             )
-            o_sb = work.tile([P, D], F32, name="o_sb_%d" % b)
-            nc.scalar.activation(out=o_sb[:], in_=o_ps[:], func=ACT.Copy, scale=inv_sum[b][:])
-            nc.sync.dma_start(out=out[b], in_=o_sb[:])
+            misc["o", b] = o_ps
+
+        def oc(b):
+            nc.scalar.activation(out=o_sb[b][:], in_=misc["o", b][:], func=ACT.Copy, scale=inv_sum[b][:])
+            nc.sync.dma_start(out=out[b], in_=o_sb[b][:])
+
+        def ocV(b):
+            nc.vector.tensor_scalar(out=o_sb[b][:], in0=misc["o", b][:], scalar1=inv_sum[b][:], scalar2=None, op0=ALU.mult)
+            nc.sync.dma_start(out=out[b], in_=o_sb[b][:])
+
+
+        Tx()
+        xc()
+        rg(0)
+        T(0, 0)
+        c(0, 0)
+        q(0, 0)
+        T(1, 0)
+        c(1, 0)
+        L(0)
+        mx(0)
+        L(1)
+        mx(1)
+        Bm()
+        bc()
+        rg(1)
+        T(0, 1)
+        ex(0)
+        q(1, 0)
+        T(1, 1)
+        c(0, 1)
+        qw(0)
+        Tp(0)
+        ex(1)
+        q(0, 1)
+        T(0, 2)
+        c(1, 1)
+        qw(1)
+        Tp(1)
+        c(0, 2)
+        rg(2)
+        T(0, 3)
+        pc(0)
+        q(1, 1)
+        T(1, 2)
+        c(0, 3)
+        qw(2)
+        T(1, 3)
+        pc(1)
+        rg(3)
+        M(0, 0)
+        c(1, 2)
+        q(0, 2)
+        M(0, 1)
+        c(1, 3)
+        qp(0)
+        M(0, 2)
+        qw(3)
+        q(0, 3)
+        M(0, 3)
+        qp(1)
+        M(1, 0)
+        q(1, 2)
+        M(1, 1)
+        rc(0)
+        M(1, 2)
+        rc(1)
+        q(1, 3)
+        M(1, 3)
+        add(0)
+        add(1)
+        qy(0)
+        C(0)
+        oc(0)
+        qy(1)
+        C(1)
+        oc(1)

@@ -109,7 +109,10 @@ def tile_mixtureexpertsmlp_pb_s_kernel(tc, h, w2, b2, x, phi, out):
         misc = {}
 
         def rg(e):
-            nc.vector.tensor_copy(out=w2_grouped[e][:], in_=w2_raw[e][:].rearrange("q g t d -> q g d t"))
+            nc.vector.tensor_copy(
+                out=w2_grouped[e][:].rearrange("q g (k i) t -> q g k t i", i=4),
+                in_=w2_raw[e][:].rearrange("q g t (k i) -> q g k t i", i=4),
+            )
 
         def rgP(e):
             nc.gpsimd.tensor_scalar(
@@ -189,8 +192,8 @@ def tile_mixtureexpertsmlp_pb_s_kernel(tc, h, w2, b2, x, phi, out):
                 in_=misc["x"][:, 0:B, :].rearrange("d j (b r) -> d b r j", b=B),
             )
             nc.scalar.copy(
-                out=xphi_t[:, B:, :].rearrange("d e (r j) -> d e r j", j=E),
-                in_=misc["x"][:, B:, :].rearrange("d j (e r) -> d e r j", e=E),
+                out=xphi_t[:, B:, :].rearrange("d e s -> d (e s)").rearrange("d (u r j c) -> d u r j c", u=HALVES, j=E, c=2),
+                in_=misc["x"][:, B:, :].rearrange("d j (u c r) -> d u r j c", u=HALVES, c=2),
             )
 
         def xcV():
@@ -234,13 +237,17 @@ def tile_mixtureexpertsmlp_pb_s_kernel(tc, h, w2, b2, x, phi, out):
             nc.vector.tensor_copy(out=bias_sb[:], in_=misc["b"][:])
 
         def Tp(b):
-            p_ps = ps_misc.tile([P, E, N], BF16, tag="misc", name="p_ps_%d" % b)
-            for e in range(E):
-                nc.tensor.transpose(p_ps[:, e, :], p_sb[b][:, e, :], ident_bf[:])
+            p_ps = ps_misc.tile([P, HALVES, N], F32, tag="misc", name="p_ps_%d" % b)
+            words = p_sb[b][:].rearrange("n e s -> n (e s)").bitcast(F32)
+            for u in range(HALVES):
+                nc.tensor.transpose(p_ps[:, u, :], words[:, u * P : (u + 1) * P], ident_f32[:])
             misc["p", b] = p_ps
 
         def pc(b):
-            nc.scalar.copy(out=p_grouped[b][:], in_=misc["p", b][:].rearrange("s e n -> s n e"))
+            nc.scalar.copy(
+                out=p_grouped[b][:].rearrange("s n t -> s (n t)").bitcast(F32).rearrange("s (n u) -> s n u", u=HALVES),
+                in_=misc["p", b][:].rearrange("s u n -> s n u"),
+            )
 
         def pcV(b):
             nc.vector.tensor_copy(out=p_grouped[b][:], in_=misc["p", b][:].rearrange("s e n -> s n e"))

@@ -54,8 +54,8 @@ def tile_mixtureexpertsmlp_pb_s_kernel(tc, h, w2, b2, x, phi, out):
         def load_w2(e):
             raw = loads.tile([P, PASSES, PACK, D], BF16, name="w2_raw_%d" % e)
             nc.sync.dma_start(
-                out=raw[:].rearrange("q g (u c) d -> q (g u) (c d)", c=2),
-                in_=w2[e].rearrange("(j q c) d -> q j (c d)", q=P, c=2),
+                out=raw[:].rearrange("q g t d -> q g (t d)"),
+                in_=w2[e].rearrange("(g q t) d -> q g (t d)", q=P, t=PACK),
             )
             w2_raw[e] = raw
 
@@ -133,8 +133,10 @@ def tile_mixtureexpertsmlp_pb_s_kernel(tc, h, w2, b2, x, phi, out):
         def T(b, e):
             words = h_sb[b, e][:].bitcast(F32)
             h_ps = ps_h.tile([P, PASSES * HALVES, S], F32, tag="h_ps")
-            for j in range(PASSES * HALVES):
-                nc.tensor.transpose(h_ps[:, j, :], words[:, j * P : (j + 1) * P], ident_f32[:])
+            for g in range(PASSES):
+                for u in range(HALVES):
+                    pass_words = words[:, HALVES * P * g + u : HALVES * P * (g + 1) : HALVES]
+                    nc.tensor.transpose(h_ps[:, HALVES * g + u, :], pass_words, ident_f32[:])
             h_banks[b, e] = h_ps
 
         def c(b, e):

from contextlib import ExitStack

import concourse.mybir as mybir
from concourse.masks import make_identity

F32 = mybir.dt.float32
BF16 = mybir.dt.bfloat16
U32 = mybir.dt.uint32
U8 = mybir.dt.uint8
FP8X4 = mybir.dt.float8_e4m3fn_x4
ALU = mybir.AluOpType
ACT = mybir.ActivationFunctionType

P = 128
B, E, S, H, D, N = 2, 4, 128, 1024, 128, 128
PACK = 4
K_PASS = P * PACK
PASSES = H // K_PASS
HALVES = 2

FLOPS = 2 * (B * E * S * H * D + B * N * D * E * S + B * N * E * S * D)


def tile_mixtureexpertsmlp_pb_s_kernel(tc, h, w2, b2, x, phi, out):
    nc = tc.nc
    with ExitStack() as ctx:
        ctx.enter_context(tc.manual_schedule())
        const = ctx.enter_context(tc.tile_pool(name="const", bufs=1))
        loads = ctx.enter_context(tc.tile_pool(name="loads", bufs=1))
        work = ctx.enter_context(tc.tile_pool(name="work", bufs=1))
        ps_h = ctx.enter_context(tc.psum_pool(name="ps_h", bufs=4))
        ps_y = ctx.enter_context(tc.psum_pool(name="ps_y", bufs=1))
        ps_misc = ctx.enter_context(tc.psum_pool(name="ps_misc", bufs=2))

        b2_rows = const.tile([P, E * D], BF16)
        nc.vector.memset(b2_rows[:].bitcast(U32), 0)
        nc.scalar.dma_start(out=b2_rows[0:1, :], in_=b2.rearrange("(o e) d -> o (e d)", o=1))
        warm = const.tile([P, 1], F32)
        nc.vector.memset(warm[:], 0.0)
        nc.scalar.activation(out=warm[:], in_=warm[:], func=ACT.Exp)
        ident_f32 = const.tile([P, P], F32)
        nc.vector.memset(ident_f32[:], 0.0)
        make_identity(nc, ident_f32[:], nomemset=True)
        ones = const.tile([P, P], BF16)
        nc.vector.memset(ones[:], 1.0)
        ident_bf = const.tile([P, P], BF16)
        nc.vector.tensor_copy(out=ident_bf[:], in_=ident_f32[:])

        w2_raw = {}
        h_sb = {}
        phi_sb = loads.tile([P, E, D], BF16)
        x_sb = loads.tile([P, B, D], BF16)

        def load_w2(e):
            raw = loads.tile([P, PASSES, PACK, D], BF16, name="w2_raw_%d" % e)
            nc.sync.dma_start(
                out=raw[:].rearrange("q g t d -> q g (t d)"),
                in_=w2[e].rearrange("(g q t) d -> q g (t d)", q=P, t=PACK),
            )
            w2_raw[e] = raw

        def load_h(b, e):
            rows = loads.tile([P, H], BF16, name="h_sb_%d_%d" % (b, e))
            nc.sync.dma_start(out=rows[:], in_=h[b, e])
            h_sb[b, e] = rows

        nc.sync.dma_start(out=phi_sb[:], in_=phi.rearrange("e s d -> (e s) d").rearrange("(q j) d -> q j d", j=E))
        nc.sync.dma_start(out=x_sb[:], in_=x.rearrange("b n d -> (b n) d").rearrange("(q j) d -> q j d", j=B))
        load_h(0, 0)
        load_h(1, 0)
        load_w2(0)
        load_h(0, 1)
        load_w2(1)
        load_h(1, 1)
        load_w2(2)
        load_h(0, 2)
        load_w2(3)
        load_h(0, 3)
        load_h(1, 2)
        load_h(1, 3)

        w2_grouped = [
            work.tile([P, PASSES, D, PACK], BF16, name="w2_grouped_%d" % e, align_bytes=64) for e in range(E)
        ]
        w2_codes = [work.tile([P, PASSES, D], U32, name="w2_codes_%d" % e, align_bytes=64) for e in range(E)]
        w2_scales = [work.tile([P, PASSES, D], U8, name="w2_scales_%d" % e, align_bytes=64) for e in range(E)]
        blocks = [(b, e) for b in range(B) for e in range(E)]
        h_grouped = {}
        h_codes = {}
        h_scales = {}
        for b, e in blocks:
            h_grouped[b, e] = work.tile([P, PASSES * S * PACK], BF16, name="h_grouped_%d_%d" % (b, e), align_bytes=64)
            h_codes[b, e] = work.tile([P, PASSES, S], U32, name="h_codes_%d_%d" % (b, e), align_bytes=64)
            h_scales[b, e] = work.tile([P, PASSES, S], U8, name="h_scales_%d_%d" % (b, e), align_bytes=64)
        y_ps = [ps_y.tile([P, E, D], F32, name="y_ps_%d" % b) for b in range(B)]
        p_sb = [work.tile([P, E, S], BF16, name="p_sb_%d" % b) for b in range(B)]
        p_grouped = [work.tile([P, N, PACK], BF16, name="p_grouped_%d" % b, align_bytes=64) for b in range(B)]
        p_codes = [work.tile([P, N], U32, name="p_codes_%d" % b, align_bytes=64) for b in range(B)]
        p_scales = [work.tile([P, N], U8, name="p_scales_%d" % b, align_bytes=64) for b in range(B)]
        bias_sb = work.tile([P, E * D], BF16)
        p_sum = [work.tile([P, 1], F32, name="p_sum_%d" % b) for b in range(B)]
        inv_sum = [work.tile([P, 1], F32, name="inv_sum_%d" % b) for b in range(B)]
        y_grouped = [work.tile([P, D, PACK], BF16, name="y_grouped_%d" % b, align_bytes=64) for b in range(B)]
        y_codes = [work.tile([P, D], U32, name="y_codes_%d" % b, align_bytes=64) for b in range(B)]
        y_scales = [work.tile([P, D], U8, name="y_scales_%d" % b, align_bytes=64) for b in range(B)]
        o_sb = [work.tile([P, D], F32, name="o_sb_%d" % b) for b in range(B)]

        h_banks = {}
        misc = {}

        def rg(e):
            nc.vector.tensor_copy(
                out=w2_grouped[e][:].rearrange("q g (k i) t -> q g k t i", i=4),
                in_=w2_raw[e][:].rearrange("q g t (k i) -> q g k t i", i=4),
            )

        def rgP(e):
            nc.gpsimd.tensor_scalar(
                out=w2_grouped[e][:], in0=w2_raw[e][:].rearrange("q g t d -> q g d t"),
                scalar1=1.0, scalar2=0.0, op0=ALU.mult, op1=ALU.add,
            )

        def rgA(e):
            nc.scalar.copy(out=w2_grouped[e][:], in_=w2_raw[e][:].rearrange("q g t d -> q g d t"))

        def qw(e):
            nc.vector.quantize_mx(
                out=w2_codes[e][:].rearrange("q g d -> q (g d)").bitcast(FP8X4),
                scales=w2_scales[e][:].rearrange("q g d -> q (g d)"),
                in_=w2_grouped[e][:].rearrange("q g d t -> q (g d t)"),
            )

        def T(b, e):
            words = h_sb[b, e][:].bitcast(F32)
            h_ps = ps_h.tile([P, PASSES * HALVES, S], F32, tag="h_ps")
            for g in range(PASSES):
                for u in range(HALVES):
                    pass_words = words[:, HALVES * P * g + u : HALVES * P * (g + 1) : HALVES]
                    nc.tensor.transpose(h_ps[:, HALVES * g + u, :], pass_words, ident_f32[:])
            h_banks[b, e] = h_ps

        def c(b, e):
            nc.scalar.copy(
                out=h_grouped[b, e][:].bitcast(F32).rearrange("q (g s u) -> q g s u", g=PASSES, u=HALVES),
                in_=h_banks[b, e][:].rearrange("q (g u) s -> q g s u", u=HALVES),
            )

        def cV(b, e):
            nc.vector.tensor_copy(
                out=h_grouped[b, e][:].bitcast(F32).rearrange("q (g s u) -> q g s u", g=PASSES, u=HALVES),
                in_=h_banks[b, e][:].rearrange("q (g u) s -> q g s u", u=HALVES),
            )

        def q(b, e):
            nc.vector.quantize_mx(
                out=h_codes[b, e][:].rearrange("q g s -> q (g s)").bitcast(FP8X4),
                scales=h_scales[b, e][:].rearrange("q g s -> q (g s)"),
                in_=h_grouped[b, e][:],
            )

        def half_T(b, e, banks):
            words = h_sb[b, e][:].bitcast(F32)
            for g in range(PASSES):
                for u in range(HALVES):
                    j = g * HALVES + u
                    nc.tensor.transpose(banks[g][:, u, :], words[:, j * P : (j + 1) * P], ident_f32[:])

        def M(b, e):
            for g in range(PASSES):
                nc.tensor.matmul_mx(
                    out=y_ps[b][:, e, :],
                    lhsT=h_codes[b, e][:, g, :].bitcast(FP8X4),
                    lhsT_scale=h_scales[b, e][:, g, :],
                    rhs=w2_codes[e][:, g, :].bitcast(FP8X4),
                    rhs_scale=w2_scales[e][:, g, :],
                    start=(g == 0),
                    stop=(g == PASSES - 1),
                )

        xphi_t = work.tile([P, B + E, P], BF16)
        neg_max = [work.tile([P, 1], F32, name="neg_max_%d" % b) for b in range(B)]

        def Tx():
            xphi_ps = ps_misc.tile([P, B + E, P], BF16, tag="misc")
            for e in range(E):
                nc.tensor.transpose(xphi_ps[:, B + e, :], phi_sb[:, e, :], ident_bf[:])
            for b in range(B):
                nc.tensor.transpose(xphi_ps[:, b, :], x_sb[:, b, :], ident_bf[:])
            misc["x"] = xphi_ps

        def xc():
            nc.scalar.copy(
                out=xphi_t[:, 0:B, :].rearrange("d b (r j) -> d b r j", j=B),
                in_=misc["x"][:, 0:B, :].rearrange("d j (b r) -> d b r j", b=B),
            )
            nc.scalar.copy(
                out=xphi_t[:, B:, :].rearrange("d e s -> d (e s)").rearrange("d (u r j c) -> d u r j c", u=HALVES, j=E, c=2),
                in_=misc["x"][:, B:, :].rearrange("d j (u c r) -> d u r j c", u=HALVES, c=2),
            )

        def xcV():
            nc.vector.tensor_copy(out=xphi_t[:], in_=misc["x"][:])

        def L(b):
            logits = ps_misc.tile([P, E * S], F32, tag="misc", name="logits_%d" % b)
            nc.tensor.matmul(
                out=logits[:],
                lhsT=xphi_t[:, b, :],
                rhs=xphi_t[:, B:, :].rearrange("d e s -> d (e s)"),
                start=True,
                stop=True,
            )
            misc["l", b] = logits

        def mx(b):
            nc.vector.tensor_reduce(
                out=neg_max[b][:], in_=misc["l", b][:], axis=mybir.AxisListType.X, op=ALU.max, negate=True
            )

        def ex(b):
            nc.scalar.activation(
                out=p_sb[b][:].rearrange("n e s -> n (e s)"),
                in_=misc["l", b][:],
                func=ACT.Exp,
                bias=neg_max[b][:],
                scale=1.0,
                accum_out=p_sum[b][:],
            )

        def Bm():
            bias_ps = ps_h.tile([P, E * D], BF16, tag="h_ps", name="bias_ps")
            nc.tensor.matmul(out=bias_ps[:], lhsT=ones[:], rhs=b2_rows[:], start=True, stop=True)
            misc["b"] = bias_ps

        def bc():
            nc.scalar.copy(out=bias_sb[:], in_=misc["b"][:])

        def bcV():
            nc.vector.tensor_copy(out=bias_sb[:], in_=misc["b"][:])

        def Tp(b):
            p_ps = ps_misc.tile([P, HALVES, N], F32, tag="misc", name="p_ps_%d" % b)
            words = p_sb[b][:].rearrange("n e s -> n (e s)").bitcast(F32)
            for u in range(HALVES):
                nc.tensor.transpose(p_ps[:, u, :], words[:, u * P : (u + 1) * P], ident_f32[:])
            misc["p", b] = p_ps

        def pc(b):
            nc.scalar.copy(
                out=p_grouped[b][:].rearrange("s n t -> s (n t)").bitcast(F32).rearrange("s (n u) -> s n u", u=HALVES),
                in_=misc["p", b][:].rearrange("s u n -> s n u"),
            )

        def pcV(b):
            nc.vector.tensor_copy(out=p_grouped[b][:], in_=misc["p", b][:].rearrange("s e n -> s n e"))

        def rc(b):
            nc.vector.reciprocal(out=inv_sum[b][:], in_=p_sum[b][:])

        def qp(b):
            nc.vector.quantize_mx(
                out=p_codes[b][:].bitcast(FP8X4),
                scales=p_scales[b][:],
                in_=p_grouped[b][:].rearrange("s n e -> s (n e)"),
            )

        def add(b):
            nc.vector.tensor_tensor(
                out=y_grouped[b][:],
                in0=y_ps[b][:].rearrange("s e d -> s d e"),
                in1=bias_sb[:].rearrange("s (e d) -> s d e", e=E),
                op=ALU.add,
            )

        def qy(b):
            nc.vector.quantize_mx(
                out=y_codes[b][:].bitcast(FP8X4),
                scales=y_scales[b][:],
                in_=y_grouped[b][:].rearrange("s d e -> s (d e)"),
            )

        def C(b):
            o_ps = ps_misc.tile([P, D], F32, tag="misc", name="o_ps_%d" % b)
            nc.tensor.matmul_mx(
                out=o_ps[:],
                lhsT=p_codes[b][:].bitcast(FP8X4),
                lhsT_scale=p_scales[b][:],
                rhs=y_codes[b][:].bitcast(FP8X4),
                rhs_scale=y_scales[b][:],
                start=True,
                stop=True,
            )
            misc["o", b] = o_ps

        def oc(b):
            nc.scalar.activation(out=o_sb[b][:], in_=misc["o", b][:], func=ACT.Copy, scale=inv_sum[b][:])
            nc.sync.dma_start(out=out[b], in_=o_sb[b][:])

        def ocV(b):
            nc.vector.tensor_scalar(out=o_sb[b][:], in0=misc["o", b][:], scalar1=inv_sum[b][:], scalar2=None, op0=ALU.mult)
            nc.sync.dma_start(out=out[b], in_=o_sb[b][:])


        Tx()
        xc()
        rg(0)
        T(0, 0)
        c(0, 0)
        q(0, 0)
        T(1, 0)
        c(1, 0)
        L(0)
        mx(0)
        L(1)
        mx(1)
        Bm()
        bc()
        rg(1)
        T(0, 1)
        ex(0)
        q(1, 0)
        T(1, 1)
        c(0, 1)
        qw(0)
        Tp(0)
        ex(1)
        q(0, 1)
        T(0, 2)
        c(1, 1)
        qw(1)
        Tp(1)
        c(0, 2)
        rg(2)
        T(0, 3)
        pc(0)
        q(1, 1)
        T(1, 2)
        c(0, 3)
        qw(2)
        T(1, 3)
        pc(1)
        rg(3)
        M(0, 0)
        c(1, 2)
        q(0, 2)
        M(0, 1)
        c(1, 3)
        qp(0)
        M(0, 2)
        qw(3)
        q(0, 3)
        M(0, 3)
        qp(1)
        M(1, 0)
        q(1, 2)
        M(1, 1)
        rc(0)
        M(1, 2)
        rc(1)
        q(1, 3)
        M(1, 3)
        add(0)
        add(1)
        qy(0)
        C(0)
        oc(0)
        qy(1)
        C(1)
        oc(1)
